import numpy as np
import ml_dtypes


def mxq(x, axis, fmt="e4m3"):
    dtype, down = {"e4m3": (ml_dtypes.float8_e4m3fn, 7), "e5m2": (ml_dtypes.float8_e5m2, 14)}[fmt]
    v = np.moveaxis(np.asarray(x, np.float32).astype(ml_dtypes.bfloat16).astype(np.float64), axis, -1)
    blocks = v.reshape(v.shape[:-1] + (-1, 32))
    amax = np.abs(blocks).max(-1, keepdims=True)
    byte = np.maximum(np.where(amax > 0, np.frexp(amax)[1] - 1 + 127, 0) - down, 1)
    scale = np.exp2(byte - 127.0)
    codes = (blocks / scale).astype(np.float32).astype(dtype).astype(np.float64)
    return np.moveaxis((codes * scale).reshape(v.shape), -1, axis)


WIDE = False


def mx_kscale(k):
    if not WIDE:
        return np.ones(k)
    levels = np.array([10, -10, 5, -5, 0])
    a = np.random.permutation(np.resize(levels, k // 512 * 4)).reshape(k // 512, 4)
    idx = np.arange(k)
    return np.exp2(a[idx // 512, idx % 128 // 32])


BF16 = ml_dtypes.bfloat16


def bf(x):
    return np.asarray(x, np.float32).astype(BF16)


def f64(x):
    return np.asarray(x).astype(np.float64)


E2M1 = np.array([0.0, 0.5, 1.0, 1.5, 2.0, 3.0, 4.0, 6.0, -0.0, -0.5, -1.0, -1.5, -2.0, -3.0, -4.0, -6.0])


def pack_weight(w, fmt):
    k, n = w.shape
    w = f64(bf(w)).reshape(k // 32, 32, n)
    amax = np.abs(w).max(1)
    if fmt == "e4m3":
        byte = np.frexp(amax)[1] - 1 + 127 - 7
    else:
        mant, ex = np.frexp(amax / 6.0)
        byte = np.where(mant > 0.5, ex, ex - 1) + 127
    byte = np.clip(np.where(amax > 0, byte, 1), 1, 254)
    scaled = (w * np.exp2(127.0 - byte)[:, None, :]).reshape(k, n).astype(np.float32)
    by_word = np.ascontiguousarray(scaled.reshape(k // 512, 128, 4, n).transpose(0, 1, 3, 2))
    if fmt == "e4m3":
        words = by_word.astype(ml_dtypes.float8_e4m3fn).view(np.uint8)
    else:
        c = by_word.astype(ml_dtypes.float4_e2m1fn).view(np.uint8) & 0xF
        words = c[..., 0::2] | (c[..., 1::2] << 4)
    return np.ascontiguousarray(words), np.ascontiguousarray(byte.astype(np.uint8).reshape(k // 512, 16, n))


def unpack_weight(words, scales, fmt):
    g, p, n, _ = words.shape
    if fmt == "e4m3":
        vals = np.ascontiguousarray(words).view(ml_dtypes.float8_e4m3fn).astype(np.float64)
    else:
        nib = np.empty((g, p, n, 4), np.uint8)
        nib[..., 0::2] = words & 0xF
        nib[..., 1::2] = words >> 4
        vals = E2M1[nib]
    vals = vals * np.repeat(np.exp2(scales.astype(np.float64) - 127.0), 8, axis=1)[..., None]
    return vals.transpose(0, 1, 3, 2).reshape(g * 512, n)

def pack4(w):
    words, scales = pack_weight(w, "e2m1")
    return words.reshape(words.shape[0], 128, -1), scales


def unpack4(words, scales):
    return unpack_weight(words.reshape(words.shape[0], 128, -1, 2), scales, "e2m1")


B, I, H, AH, AI, G = 512, 1024, 1024, 128, 128, 4
EPS = 1e-5
K = I + H


def sigmoid(v):
    return 1.0 / (1.0 + np.exp(-v))


def ln(v, w, b):
    mu = v.mean(-1, keepdims=True)
    var = ((v - mu) ** 2).mean(-1, keepdims=True)
    return (v - mu) / np.sqrt(var + EPS) * w + b


def setup_inputs():
    n = np.random.standard_normal
    s = mx_kscale(K)
    x = bf(n((B, I)) * s[:I])
    hx = bf(n((B, H)) * s[I:])
    ah = bf(n((B, AH)))
    ac = bf(n((B, AH)))
    a_w_ih_words, a_w_ih_scales = pack4((n((G * AH, K)) / np.sqrt(K) / s).T)
    return {
        "x": x,
        "hx": hx,
        "ah": ah,
        "ac": ac,
        "a_w_ih_words": a_w_ih_words,
        "a_w_ih_scales": a_w_ih_scales,
        "a_w_hh": bf(n((G * AH, AH)) / np.sqrt(AH)),
        "a_ln_i_w": bf(1.0 + 0.1 * n(G * AH)),
        "a_ln_i_b": bf(0.2 * n(G * AH)),
        "a_ln_h_w": bf(1.0 + 0.1 * n(G * AH)),
        "a_ln_h_b": bf(0.2 * n(G * AH)),
        "a_ln_c_w": bf(1.0 + 0.1 * n(AH)),
        "a_ln_c_b": bf(0.2 * n(AH)),
    }


def reference(x, hx, ah, ac, a_w_ih_words, a_w_ih_scales, a_w_hh, a_ln_i_w, a_ln_i_b, a_ln_h_w, a_ln_h_b, a_ln_c_w, a_ln_c_b):
    ai = np.concatenate([f64(x), f64(hx)], axis=1)
    ig = ln(mxq(ai, 1, "e4m3") @ unpack4(a_w_ih_words, a_w_ih_scales), f64(a_ln_i_w), f64(a_ln_i_b))
    hg = ln(f64(ah) @ f64(a_w_hh).T, f64(a_ln_h_w), f64(a_ln_h_b))
    g = ig + hg
    gi, gf, gj, go = np.split(g, G, axis=1)
    acy = ln(sigmoid(gf) * f64(ac) + sigmoid(gi) * np.tanh(gj), f64(a_ln_c_w), f64(a_ln_c_b))
    ada = sigmoid(go) * np.tanh(acy)
    return ada, acy

@@ -1,0 +1,354 @@
+import concourse.mybir as mybir
+from concourse.masks import make_identity
+
+F32 = mybir.dt.float32
+BF16 = mybir.dt.bfloat16
+I32 = mybir.dt.int32
+U32 = mybir.dt.uint32
+U8 = mybir.dt.uint8
+FP8X4 = mybir.dt.float8_e4m3fn_x4
+FP4X4 = mybir.dt.float4_e2m1fn_x4
+ALU = mybir.AluOpType
+ACT = mybir.ActivationFunctionType
+
+P = 128
+BATCH = 512
+TILES = BATCH // P
+IN = 1024
+K = 2 * IN
+K_PASS = 512
+PASSES = K // K_PASS
+AH = 128
+GATES = 4 * AH
+EPS = 1e-5
+
+FLOPS = 2 * BATCH * GATES * K + 2 * BATCH * GATES * AH
+
+
+def tile_adaptivelstmcell_pa_kernel(
+    tc, x, hx, ah, ac, a_w_ih_words, a_w_ih_scales, a_w_hh,
+    a_ln_i_w, a_ln_i_b, a_ln_h_w, a_ln_h_b, a_ln_c_w, a_ln_c_b, out_0, out_1,
+):
+    nc = tc.nc
+    with tc.tile_pool(name="keep", bufs=1) as keep, \
+            tc.tile_pool(name="rows", bufs=TILES) as rows, \
+            tc.tile_pool(name="work", bufs=3) as work, \
+            tc.psum_pool(name="fixed", bufs=1) as fixed, \
+            tc.psum_pool(name="psum", bufs=2) as psum, \
+            tc.manual_schedule():
+
+        ident_bf16 = keep.tile([P, P], BF16)
+        make_identity(nc, ident_bf16[:])
+        ident_f32 = keep.tile([P, P], F32)
+        make_identity(nc, ident_f32[:])
+        neg_half = keep.tile([P, TILES], F32)
+        nc.vector.memset(neg_half[:], -0.5)
+        ones = keep.tile([P, P], BF16)
+        nc.vector.memset(ones[:], 1.0)
+
+        whh_sb = keep.tile([P, 4, AH], BF16)
+        nc.scalar.dma_start(out=whh_sb[:], in_=a_w_hh.rearrange("(c p) k -> p c k", p=P))
+        ah_sb = keep.tile([P, TILES, AH], BF16)
+        nc.scalar.dma_start(out=ah_sb[:], in_=ah.rearrange("(p t) k -> p t k", t=TILES))
+
+        vec_rows = keep.tile([P, 3, GATES], BF16)
+        nc.vector.memset(vec_rows[:], 0.0)
+        for row, block, vec in ((0, 0, a_ln_h_w), (0, 2, a_ln_i_b), (1, 2, a_ln_h_b), (0, 1, a_ln_i_w)):
+            nc.scalar.dma_start(
+                out=vec_rows[row : row + 1, block, :], in_=vec.rearrange("(r c) -> r c", r=1)
+            )
+
+        x_rows = x.rearrange("(p t) k -> p t k", t=TILES)
+        hx_rows = hx.rearrange("(p t) k -> p t k", t=TILES)
+        ai_sb = []
+        for t in range(TILES):
+            ai_sb.append(rows.tile([P, K], BF16, name="ai_sb"))
+
+        def load_ai(t):
+            nc.sync.dma_start(out=ai_sb[t][:, 0:IN], in_=x_rows[:, t, :])
+            nc.sync.dma_start(out=ai_sb[t][:, IN:K], in_=hx_rows[:, t, :])
+
+        load_ai(0)
+        w_planes = keep.tile([P, PASSES, GATES], U8, align_bytes=64)
+        nc.vector.memset(w_planes[:].bitcast(I32), 0)
+        scale_rows = a_w_ih_scales.bitcast(I32)
+        for quad in range(4):
+            nc.sync.dma_start(
+                out=w_planes[32 * quad : 32 * quad + 4, :, :].bitcast(I32),
+                in_=scale_rows[:, 4 * quad : 4 * quad + 4, :].rearrange("g r n -> r g n"),
+            )
+        w_sb = keep.tile([P, PASSES, 2 * GATES], U8, align_bytes=64)
+        nc.sync.dma_start(
+            out=w_sb[:].bitcast(I32),
+            in_=a_w_ih_words.bitcast(I32).rearrange("g p n -> p g n"),
+        )
+        for t in range(1, TILES):
+            load_ai(t)
+
+        cell_rows = keep.tile([P, P], BF16)
+        nc.vector.memset(cell_rows[:], 0.0)
+        for row, vec in ((0, a_ln_c_w), (1, a_ln_c_b)):
+            nc.gpsimd.dma_start(
+                out=cell_rows[row : row + 1, :], in_=vec.rearrange("(r c) -> r c", r=1)
+            )
+        ac_sb = keep.tile([P, TILES, AH], BF16)
+        nc.gpsimd.dma_start(out=ac_sb[:], in_=ac.rearrange("(p t) n -> p t n", t=TILES))
+
+        warm = keep.tile([P, 1], F32)
+        nc.scalar.activation(out=warm[:], in_=neg_half[:, 0:1], func=ACT.Sigmoid)
+
+        whhT_ps = psum.tile([P, 4, AH], BF16, tag="ig")
+        for c in range(4):
+            nc.tensor.transpose(whhT_ps[:, c, :], whh_sb[:, c, :], ident_bf16[:])
+        ahT_ps = psum.tile([P, TILES, P], BF16, tag="ig")
+        for t in range(TILES):
+            nc.tensor.transpose(ahT_ps[:, t, :], ah_sb[:, t, :], ident_bf16[:])
+        whhT = keep.tile([P, GATES], BF16)
+        nc.vector.tensor_copy(out=whhT[:], in_=whhT_ps[:].rearrange("p c n -> p (c n)"))
+        ahT = keep.tile([P, TILES, P], BF16)
+        nc.scalar.copy(out=ahT[:], in_=ahT_ps[:])
+
+        def spread(out, block):
+            nc.tensor.matmul(out=out, lhsT=ones[:], rhs=vec_rows[:, block, :], start=True, stop=True)
+
+        def rstd_of(var_eps, width, name):
+            rstd = keep.tile([P, width], F32, name=name)
+            nc.gpsimd.tensor_tensor(out=rstd[:], in0=var_eps, in1=neg_half[:, 0:width], op=ALU.pow)
+            return rstd
+
+        def tiles_of(pair):
+            return (2 * pair, 2 * pair + 1)
+
+        hg_ps = {}
+        hg_stats = keep.tile([P, TILES, 6], F32)
+        hg_mean_var = keep.tile([P, TILES, 2], F32)
+        hg_centred = keep.tile([P, TILES, GATES], F32)
+        hidden = keep.tile([P, TILES, GATES], F32)
+
+        def hidden_product(pair):
+            for t in tiles_of(pair):
+                hg_ps[t] = psum.tile([P, GATES], F32, tag="hg", name="hg_ps")
+                nc.tensor.matmul(
+                    out=hg_ps[t][:], lhsT=ahT[:, t, :], rhs=whhT[:], start=True, stop=True
+                )
+
+        def hidden_statistics(pair):
+            for t in tiles_of(pair):
+                nc.vector.bn_stats(out=hg_stats[:, t, :], in_=hg_ps[t][:])
+            for t in tiles_of(pair):
+                nc.vector.bn_aggr(out=hg_mean_var[:, t, :], in_=hg_stats[:, t, :])
+
+        def hidden_centre(pair):
+            for t in tiles_of(pair):
+                nc.vector.scalar_tensor_tensor(
+                    out=hg_centred[:, t, :], in0=hg_ps[t][:], scalar=hg_mean_var[:, t, 0:1],
+                    in1=gain_h[:], op0=ALU.subtract, op1=ALU.mult,
+                )
+
+        def hidden_finish(t):
+            nc.vector.scalar_tensor_tensor(
+                out=hidden[:, t, :], in0=hg_centred[:, t, :], scalar=hg_rstd[:, t : t + 1],
+                in1=shift_ps[:], op0=ALU.mult, op1=ALU.add,
+            )
+
+        grouped = {}
+        ig_ps = {}
+        ig = keep.tile([P, TILES, GATES], F32)
+        ig_total = keep.tile([P, TILES], F32)
+        ig_neg_mean = keep.tile([P, TILES], F32)
+        ig_square_total = keep.tile([P, TILES], F32)
+        ig_var_eps = keep.tile([P, TILES], F32)
+        ig_rstd = {}
+
+        def flip(t):
+            grouped[t] = rows.tile([P, PASSES, P, 4], BF16, name="grouped", align_bytes=64)
+            pairs = ai_sb[t][:].bitcast(F32)
+            for half in range(2):
+                flipped = psum.tile([P, 2, 2, P], F32, tag="flipped")
+                for g2 in range(2):
+                    g = 2 * half + g2
+                    for u in range(2):
+                        nc.tensor.transpose(
+                            flipped[:, g2, u, :],
+                            pairs[:, 256 * g + u : 256 * (g + 1) : 2],
+                            ident_f32[:],
+                        )
+                nc.scalar.copy(
+                    out=grouped[t][:, 2 * half : 2 * half + 2, :, :]
+                    .rearrange("p g b t -> p (g b t)").bitcast(F32)
+                    .rearrange("p (g b u) -> p g b u", g=2, u=2),
+                    in_=flipped[:].rearrange("p g u b -> p g b u"),
+                )
+
+        def input_product(t):
+            codes = rows.tile([P, PASSES, P], U32, name="codes", align_bytes=64)
+            planes = rows.tile([P, PASSES, P], U8, name="planes", align_bytes=64)
+            nc.vector.quantize_mx(
+                out=codes[:].rearrange("p g b -> p (g b)").bitcast(FP8X4),
+                scales=planes[:].rearrange("p g b -> p (g b)"),
+                in_=grouped[t][:].rearrange("p g b t -> p (g b t)"),
+            )
+            ig_ps[t] = psum.tile([P, GATES], F32, tag="ig", name="ig_ps")
+            for g in range(PASSES):
+                nc.tensor.matmul_mx(
+                    out=ig_ps[t][:],
+                    lhsT=codes[:, g, :].bitcast(FP8X4),
+                    lhsT_scale=planes[:, g, :],
+                    rhs=w_sb[:, g, :].bitcast(FP4X4),
+                    rhs_scale=w_planes[:, g, :],
+                    start=(g == 0),
+                    stop=(g == PASSES - 1),
+                )
+
+        def input_statistics(pair):
+            both = slice(2 * pair, 2 * pair + 2)
+            for t in tiles_of(pair):
+                nc.scalar.activation(
+                    out=ig[:, t, :], in_=ig_ps[t][:], func=ACT.Identity,
+                    accum_out=ig_total[:, t : t + 1],
+                )
+            nc.scalar.mul(out=ig_neg_mean[:, both], in_=ig_total[:, both], mul=-1.0 / GATES)
+            for t in tiles_of(pair):
+                squares = work.tile([P, GATES], F32, name="ig_squares")
+                nc.scalar.activation(
+                    out=squares[:], in_=ig[:, t, :], func=ACT.Square,
+                    bias=ig_neg_mean[:, t : t + 1], accum_out=ig_square_total[:, t : t + 1],
+                )
+            nc.scalar.activation(
+                out=ig_var_eps[:, both], in_=ig_square_total[:, both], func=ACT.Copy,
+                scale=1.0 / GATES, bias=EPS,
+            )
+            ig_rstd[pair] = rstd_of(ig_var_eps[:, both], 2, "ig_rstd%d" % pair)
+
+        ig_centred = keep.tile([P, TILES, GATES], F32)
+        pre = keep.tile([P, TILES, GATES], F32)
+        in_forget = keep.tile([P, TILES, 2 * AH], F32)
+        candidate = keep.tile([P, TILES, AH], F32)
+        out_gate = keep.tile([P, TILES, AH], F32)
+        kept = keep.tile([P, TILES, AH], F32)
+        fresh = keep.tile([P, TILES, AH], F32)
+        raw = keep.tile([P, TILES, AH], F32)
+        cell_stats = keep.tile([P, TILES, 6], F32)
+        cell_mean_var = keep.tile([P, TILES, 2], F32)
+        cell_var_eps = keep.tile([P, TILES], F32)
+        cell_rstd = {}
+        cell_centred = keep.tile([P, TILES, AH], F32)
+        acy = keep.tile([P, TILES, AH], F32)
+        squashed = keep.tile([P, TILES, AH], F32)
+        ada = keep.tile([P, TILES, AH], F32)
+        ada_rows = out_0.rearrange("(p t) n -> p t n", t=TILES)
+        acy_rows = out_1.rearrange("(p t) n -> p t n", t=TILES)
+
+        def gates(pair):
+            both = slice(2 * pair, 2 * pair + 2)
+            for t in tiles_of(pair):
+                nc.vector.scalar_tensor_tensor(
+                    out=ig_centred[:, t, :], in0=ig[:, t, :], scalar=ig_neg_mean[:, t : t + 1],
+                    in1=gains_ps[:, 0:GATES], op0=ALU.add, op1=ALU.mult,
+                )
+            for t in tiles_of(pair):
+                nc.vector.scalar_tensor_tensor(
+                    out=pre[:, t, :], in0=ig_centred[:, t, :],
+                    scalar=ig_rstd[pair][:, t - 2 * pair : t - 2 * pair + 1],
+                    in1=hidden[:, t, :], op0=ALU.mult, op1=ALU.add,
+                )
+            nc.scalar.activation(
+                out=in_forget[:, both, :], in_=pre[:, both, 0 : 2 * AH], func=ACT.Sigmoid
+            )
+            nc.scalar.activation(
+                out=candidate[:, both, :], in_=pre[:, both, 2 * AH : 3 * AH], func=ACT.Tanh
+            )
+            nc.scalar.activation(
+                out=out_gate[:, both, :], in_=pre[:, both, 3 * AH : 4 * AH], func=ACT.Sigmoid
+            )
+
+        def new_cell(pair):
+            both = slice(2 * pair, 2 * pair + 2)
+            nc.vector.tensor_mul(
+                out=kept[:, both, :], in0=in_forget[:, both, AH : 2 * AH], in1=ac_sb[:, both, :]
+            )
+            nc.vector.tensor_mul(
+                out=fresh[:, both, :], in0=in_forget[:, both, 0:AH], in1=candidate[:, both, :]
+            )
+            nc.vector.tensor_add(out=raw[:, both, :], in0=kept[:, both, :], in1=fresh[:, both, :])
+            for t in tiles_of(pair):
+                nc.vector.bn_stats(out=cell_stats[:, t, :], in_=raw[:, t, :])
+            for t in tiles_of(pair):
+                nc.vector.bn_aggr(out=cell_mean_var[:, t, :], in_=cell_stats[:, t, :])
+            nc.vector.tensor_scalar_add(
+                out=cell_var_eps[:, both], in0=cell_mean_var[:, both, 1], scalar1=EPS
+            )
+            cell_rstd[pair] = rstd_of(cell_var_eps[:, both], 2, "cell_rstd%d" % pair)
+            for t in tiles_of(pair):
+                nc.vector.scalar_tensor_tensor(
+                    out=cell_centred[:, t, :], in0=raw[:, t, :], scalar=cell_mean_var[:, t, 0:1],
+                    in1=gains_ps[:, GATES : GATES + AH], op0=ALU.subtract, op1=ALU.mult,
+                )
+
+        def cell_output(pair):
+            both = slice(2 * pair, 2 * pair + 2)
+            for t in tiles_of(pair):
+                nc.vector.scalar_tensor_tensor(
+                    out=acy[:, t, :], in0=cell_centred[:, t, :],
+                    scalar=cell_rstd[pair][:, t - 2 * pair : t - 2 * pair + 1],
+                    in1=gains_ps[:, GATES + AH : GATES + 2 * AH], op0=ALU.mult, op1=ALU.add,
+                )
+            nc.sync.dma_start(out=acy_rows[:, both, :], in_=acy[:, both, :])
+            nc.scalar.activation(out=squashed[:, both, :], in_=acy[:, both, :], func=ACT.Tanh)
+
+        def hidden_output(pair):
+            both = slice(2 * pair, 2 * pair + 2)
+            nc.vector.tensor_mul(
+                out=ada[:, both, :], in0=out_gate[:, both, :], in1=squashed[:, both, :]
+            )
+            nc.sync.dma_start(out=ada_rows[:, both, :], in_=ada[:, both, :])
+
+        hidden_product(0)
+        gain_h_ps = psum.tile([P, GATES], BF16, tag="ig")
+        spread(gain_h_ps[:], 0)
+        flip(0)
+        hidden_statistics(0)
+        gain_h = keep.tile([P, GATES], BF16)
+        nc.vector.tensor_copy(out=gain_h[:], in_=gain_h_ps[:])
+        hidden_centre(0)
+        hidden_product(1)
+        gains_ps = fixed.tile([P, GATES + 2 * AH], BF16)
+        spread(gains_ps[:, 0:GATES], 1)
+        shift_ps = fixed.tile([P, GATES], F32)
+        spread(shift_ps[:], 2)
+        flip(1)
+        flip(2)
+        input_product(0)
+        hidden_statistics(1)
+        hg_var_eps = keep.tile([P, TILES], F32)
+        nc.vector.tensor_scalar_add(out=hg_var_eps[:], in0=hg_mean_var[:, :, 1], scalar1=EPS)
+        hg_rstd = rstd_of(hg_var_eps[:], TILES, "hg_rstd")
+        hidden_centre(1)
+        flip(3)
+        input_product(1)
+        input_statistics(0)
+        input_product(2)
+        input_product(3)
+        input_statistics(1)
+        for t in range(TILES):
+            hidden_finish(t)
+
+        cell_cols_ps = psum.tile([P, P], BF16, tag="hg")
+        nc.tensor.transpose(cell_cols_ps[:], cell_rows[:], ident_bf16[:])
+        cell_cols = keep.tile([P, 2], BF16)
+        nc.vector.tensor_copy(out=cell_cols[:], in_=cell_cols_ps[:, 0:2])
+        for c in range(2):
+            nc.tensor.transpose(
+                gains_ps[:, GATES + c * AH : GATES + (c + 1) * AH],
+                cell_cols[:, c : c + 1].to_broadcast([P, P]),
+                ident_bf16[:],
+            )
+
+        for pair in range(2):
+            gates(pair)
+        for pair in range(2):
+            new_cell(pair)
+        for pair in range(2):
+            cell_output(pair)
+        for pair in range(2):
+            hidden_output(pair)

@@ -33,15 +33,15 @@ def tile_adaptivelstmcell_pa_kernel(
     with tc.tile_pool(name="keep", bufs=1) as keep, \
             tc.tile_pool(name="rows", bufs=TILES) as rows, \
             tc.tile_pool(name="work", bufs=3) as work, \
-            tc.psum_pool(name="fixed", bufs=1) as fixed, \
-            tc.psum_pool(name="psum", bufs=2) as psum, \
+            tc.psum_pool(name="turn", bufs=2) as turn, \
+            tc.psum_pool(name="psum", bufs=6) as psum, \
             tc.manual_schedule():
 
         ident_bf16 = keep.tile([P, P], BF16)
         make_identity(nc, ident_bf16[:])
         ident_f32 = keep.tile([P, P], F32)
         make_identity(nc, ident_f32[:])
-        neg_half = keep.tile([P, TILES], F32)
+        neg_half = keep.tile([P, 2], F32)
         nc.vector.memset(neg_half[:], -0.5)
         ones = keep.tile([P, P], BF16)
         nc.vector.memset(ones[:], 1.0)
@@ -97,10 +97,10 @@ def tile_adaptivelstmcell_pa_kernel(
         warm = keep.tile([P, 1], F32)
         nc.scalar.activation(out=warm[:], in_=neg_half[:, 0:1], func=ACT.Sigmoid)
 
-        whhT_ps = psum.tile([P, 4, AH], BF16, tag="ig")
+        whhT_ps = psum.tile([P, 4, AH], BF16, tag="bank")
         for c in range(4):
             nc.tensor.transpose(whhT_ps[:, c, :], whh_sb[:, c, :], ident_bf16[:])
-        ahT_ps = psum.tile([P, TILES, P], BF16, tag="ig")
+        ahT_ps = psum.tile([P, TILES, P], BF16, tag="bank")
         for t in range(TILES):
             nc.tensor.transpose(ahT_ps[:, t, :], ah_sb[:, t, :], ident_bf16[:])
         whhT = keep.tile([P, GATES], BF16)
@@ -111,32 +111,40 @@ def tile_adaptivelstmcell_pa_kernel(
         def spread(out, block):
             nc.tensor.matmul(out=out, lhsT=ones[:], rhs=vec_rows[:, block, :], start=True, stop=True)
 
-        def rstd_of(var_eps, width, name):
-            rstd = keep.tile([P, width], F32, name=name)
-            nc.gpsimd.tensor_tensor(out=rstd[:], in0=var_eps, in1=neg_half[:, 0:width], op=ALU.pow)
+        def rstd_of(squares, scale, name):
+            var_eps = keep.tile([P, 2], F32, name=name + "_var_eps")
+            nc.gpsimd.tensor_scalar(
+                out=var_eps[:], in0=squares, scalar1=scale, scalar2=EPS, op0=ALU.mult, op1=ALU.add
+            )
+            rstd = keep.tile([P, 2], F32, name=name)
+            nc.gpsimd.tensor_tensor(out=rstd[:], in0=var_eps[:], in1=neg_half[:], op=ALU.pow)
             return rstd
 
         def tiles_of(pair):
             return (2 * pair, 2 * pair + 1)
 
+        def both(pair):
+            return slice(2 * pair, 2 * pair + 2)
+
         hg_ps = {}
         hg_stats = keep.tile([P, TILES, 6], F32)
         hg_mean_var = keep.tile([P, TILES, 2], F32)
+        hg_rstd = {}
         hg_centred = keep.tile([P, TILES, GATES], F32)
         hidden = keep.tile([P, TILES, GATES], F32)
 
-        def hidden_product(pair):
+        def hidden_product(t):
+            hg_ps[t] = psum.tile([P, GATES], F32, tag="bank", name="hg_ps")
+            nc.tensor.matmul(out=hg_ps[t][:], lhsT=ahT[:, t, :], rhs=whhT[:], start=True, stop=True)
+
+        def hidden_sums(pair):
             for t in tiles_of(pair):
-                hg_ps[t] = psum.tile([P, GATES], F32, tag="hg", name="hg_ps")
-                nc.tensor.matmul(
-                    out=hg_ps[t][:], lhsT=ahT[:, t, :], rhs=whhT[:], start=True, stop=True
-                )
+                nc.vector.bn_stats(out=hg_stats[:, t, :], in_=hg_ps[t][:])
 
         def hidden_statistics(pair):
             for t in tiles_of(pair):
-                nc.vector.bn_stats(out=hg_stats[:, t, :], in_=hg_ps[t][:])
-            for t in tiles_of(pair):
                 nc.vector.bn_aggr(out=hg_mean_var[:, t, :], in_=hg_stats[:, t, :])
+            hg_rstd[pair] = rstd_of(hg_mean_var[:, both(pair), 1], 1.0, "hg_rstd%d" % pair)
 
         def hidden_centre(pair):
             for t in tiles_of(pair):
@@ -145,26 +153,27 @@ def tile_adaptivelstmcell_pa_kernel(
                     in1=gain_h[:], op0=ALU.subtract, op1=ALU.mult,
                 )
 
-        def hidden_finish(t):
-            nc.vector.scalar_tensor_tensor(
-                out=hidden[:, t, :], in0=hg_centred[:, t, :], scalar=hg_rstd[:, t : t + 1],
-                in1=shift_ps[:], op0=ALU.mult, op1=ALU.add,
-            )
+        def hidden_finish(pair):
+            for t in tiles_of(pair):
+                nc.vector.scalar_tensor_tensor(
+                    out=hidden[:, t, :], in0=hg_centred[:, t, :],
+                    scalar=hg_rstd[pair][:, t % 2 : t % 2 + 1],
+                    in1=shift_ps[:], op0=ALU.mult, op1=ALU.add,
+                )
 
         grouped = {}
+        codes = {}
+        planes = {}
         ig_ps = {}
-        ig = keep.tile([P, TILES, GATES], F32)
-        ig_total = keep.tile([P, TILES], F32)
         ig_neg_mean = keep.tile([P, TILES], F32)
-        ig_square_total = keep.tile([P, TILES], F32)
-        ig_var_eps = keep.tile([P, TILES], F32)
+        ig_squares = keep.tile([P, TILES], F32)
         ig_rstd = {}
 
         def flip(t):
             grouped[t] = rows.tile([P, PASSES, P, 4], BF16, name="grouped", align_bytes=64)
             pairs = ai_sb[t][:].bitcast(F32)
             for half in range(2):
-                flipped = psum.tile([P, 2, 2, P], F32, tag="flipped")
+                flipped = turn.tile([P, 2, 2, P], F32)
                 for g2 in range(2):
                     g = 2 * half + g2
                     for u in range(2):
@@ -180,45 +189,44 @@ def tile_adaptivelstmcell_pa_kernel(
                     in_=flipped[:].rearrange("p g u b -> p g b u"),
                 )
 
-        def input_product(t):
-            codes = rows.tile([P, PASSES, P], U32, name="codes", align_bytes=64)
-            planes = rows.tile([P, PASSES, P], U8, name="planes", align_bytes=64)
+        def quantise(t):
+            codes[t] = rows.tile([P, PASSES, P], U32, name="codes", align_bytes=64)
+            planes[t] = rows.tile([P, PASSES, P], U8, name="planes", align_bytes=64)
             nc.vector.quantize_mx(
-                out=codes[:].rearrange("p g b -> p (g b)").bitcast(FP8X4),
-                scales=planes[:].rearrange("p g b -> p (g b)"),
+                out=codes[t][:].rearrange("p g b -> p (g b)").bitcast(FP8X4),
+                scales=planes[t][:].rearrange("p g b -> p (g b)"),
                 in_=grouped[t][:].rearrange("p g b t -> p (g b t)"),
             )
-            ig_ps[t] = psum.tile([P, GATES], F32, tag="ig", name="ig_ps")
+
+        def input_product(t):
+            ig_ps[t] = psum.tile([P, GATES], F32, tag="bank", name="ig_ps")
             for g in range(PASSES):
                 nc.tensor.matmul_mx(
                     out=ig_ps[t][:],
-                    lhsT=codes[:, g, :].bitcast(FP8X4),
-                    lhsT_scale=planes[:, g, :],
+                    lhsT=codes[t][:, g, :].bitcast(FP8X4),
+                    lhsT_scale=planes[t][:, g, :],
                     rhs=w_sb[:, g, :].bitcast(FP4X4),
                     rhs_scale=w_planes[:, g, :],
                     start=(g == 0),
                     stop=(g == PASSES - 1),
                 )
 
-        def input_statistics(pair):
-            both = slice(2 * pair, 2 * pair + 2)
+        def input_means(pair):
             for t in tiles_of(pair):
+                unused = work.tile([P, GATES], F32, name="unused")
                 nc.scalar.activation(
-                    out=ig[:, t, :], in_=ig_ps[t][:], func=ACT.Identity,
-                    accum_out=ig_total[:, t : t + 1],
+                    out=unused[:], in_=ig_ps[t][:], func=ACT.Identity, scale=-1.0 / GATES,
+                    accum_out=ig_neg_mean[:, t : t + 1],
                 )
-            nc.scalar.mul(out=ig_neg_mean[:, both], in_=ig_total[:, both], mul=-1.0 / GATES)
+
+        def input_deviations(pair):
             for t in tiles_of(pair):
-                squares = work.tile([P, GATES], F32, name="ig_squares")
+                unused = work.tile([P, GATES], F32, name="unused")
                 nc.scalar.activation(
-                    out=squares[:], in_=ig[:, t, :], func=ACT.Square,
-                    bias=ig_neg_mean[:, t : t + 1], accum_out=ig_square_total[:, t : t + 1],
+                    out=unused[:], in_=ig_ps[t][:], func=ACT.Square, bias=ig_neg_mean[:, t : t + 1],
+                    accum_out=ig_squares[:, t : t + 1],
                 )
-            nc.scalar.activation(
-                out=ig_var_eps[:, both], in_=ig_square_total[:, both], func=ACT.Copy,
-                scale=1.0 / GATES, bias=EPS,
-            )
-            ig_rstd[pair] = rstd_of(ig_var_eps[:, both], 2, "ig_rstd%d" % pair)
+            ig_rstd[pair] = rstd_of(ig_squares[:, both(pair)], 1.0 / GATES, "ig_rstd%d" % pair)
 
         ig_centred = keep.tile([P, TILES, GATES], F32)
         pre = keep.tile([P, TILES, GATES], F32)
@@ -230,7 +238,6 @@ def tile_adaptivelstmcell_pa_kernel(
         raw = keep.tile([P, TILES, AH], F32)
         cell_stats = keep.tile([P, TILES, 6], F32)
         cell_mean_var = keep.tile([P, TILES, 2], F32)
-        cell_var_eps = keep.tile([P, TILES], F32)
         cell_rstd = {}
         cell_centred = keep.tile([P, TILES, AH], F32)
         acy = keep.tile([P, TILES, AH], F32)
@@ -240,45 +247,42 @@ def tile_adaptivelstmcell_pa_kernel(
         acy_rows = out_1.rearrange("(p t) n -> p t n", t=TILES)
 
         def gates(pair):
-            both = slice(2 * pair, 2 * pair + 2)
             for t in tiles_of(pair):
                 nc.vector.scalar_tensor_tensor(
-                    out=ig_centred[:, t, :], in0=ig[:, t, :], scalar=ig_neg_mean[:, t : t + 1],
-                    in1=gains_ps[:, 0:GATES], op0=ALU.add, op1=ALU.mult,
+                    out=ig_centred[:, t, :], in0=ig_ps[t][:], scalar=ig_neg_mean[:, t : t + 1],
+                    in1=gain_i[:], op0=ALU.add, op1=ALU.mult,
                 )
             for t in tiles_of(pair):
                 nc.vector.scalar_tensor_tensor(
                     out=pre[:, t, :], in0=ig_centred[:, t, :],
-                    scalar=ig_rstd[pair][:, t - 2 * pair : t - 2 * pair + 1],
+                    scalar=ig_rstd[pair][:, t % 2 : t % 2 + 1],
                     in1=hidden[:, t, :], op0=ALU.mult, op1=ALU.add,
                 )
+            two = both(pair)
             nc.scalar.activation(
-                out=in_forget[:, both, :], in_=pre[:, both, 0 : 2 * AH], func=ACT.Sigmoid
+                out=in_forget[:, two, :], in_=pre[:, two, 0 : 2 * AH], func=ACT.Sigmoid
             )
             nc.scalar.activation(
-                out=candidate[:, both, :], in_=pre[:, both, 2 * AH : 3 * AH], func=ACT.Tanh
+                out=candidate[:, two, :], in_=pre[:, two, 2 * AH : 3 * AH], func=ACT.Tanh
             )
             nc.scalar.activation(
-                out=out_gate[:, both, :], in_=pre[:, both, 3 * AH : 4 * AH], func=ACT.Sigmoid
+                out=out_gate[:, two, :], in_=pre[:, two, 3 * AH : 4 * AH], func=ACT.Sigmoid
             )
 
         def new_cell(pair):
-            both = slice(2 * pair, 2 * pair + 2)
+            two = both(pair)
             nc.vector.tensor_mul(
-                out=kept[:, both, :], in0=in_forget[:, both, AH : 2 * AH], in1=ac_sb[:, both, :]
+                out=kept[:, two, :], in0=in_forget[:, two, AH : 2 * AH], in1=ac_sb[:, two, :]
             )
             nc.vector.tensor_mul(
-                out=fresh[:, both, :], in0=in_forget[:, both, 0:AH], in1=candidate[:, both, :]
+                out=fresh[:, two, :], in0=in_forget[:, two, 0:AH], in1=candidate[:, two, :]
             )
-            nc.vector.tensor_add(out=raw[:, both, :], in0=kept[:, both, :], in1=fresh[:, both, :])
+            nc.vector.tensor_add(out=raw[:, two, :], in0=kept[:, two, :], in1=fresh[:, two, :])
             for t in tiles_of(pair):
                 nc.vector.bn_stats(out=cell_stats[:, t, :], in_=raw[:, t, :])
             for t in tiles_of(pair):
                 nc.vector.bn_aggr(out=cell_mean_var[:, t, :], in_=cell_stats[:, t, :])
-            nc.vector.tensor_scalar_add(
-                out=cell_var_eps[:, both], in0=cell_mean_var[:, both, 1], scalar1=EPS
-            )
-            cell_rstd[pair] = rstd_of(cell_var_eps[:, both], 2, "cell_rstd%d" % pair)
+            cell_rstd[pair] = rstd_of(cell_mean_var[:, two, 1], 1.0, "cell_rstd%d" % pair)
             for t in tiles_of(pair):
                 nc.vector.scalar_tensor_tensor(
                     out=cell_centred[:, t, :], in0=raw[:, t, :], scalar=cell_mean_var[:, t, 0:1],
@@ -286,54 +290,65 @@ def tile_adaptivelstmcell_pa_kernel(
                 )
 
         def cell_output(pair):
-            both = slice(2 * pair, 2 * pair + 2)
+            two = both(pair)
             for t in tiles_of(pair):
                 nc.vector.scalar_tensor_tensor(
                     out=acy[:, t, :], in0=cell_centred[:, t, :],
-                    scalar=cell_rstd[pair][:, t - 2 * pair : t - 2 * pair + 1],
+                    scalar=cell_rstd[pair][:, t % 2 : t % 2 + 1],
                     in1=gains_ps[:, GATES + AH : GATES + 2 * AH], op0=ALU.mult, op1=ALU.add,
                 )
-            nc.sync.dma_start(out=acy_rows[:, both, :], in_=acy[:, both, :])
-            nc.scalar.activation(out=squashed[:, both, :], in_=acy[:, both, :], func=ACT.Tanh)
+            nc.sync.dma_start(out=acy_rows[:, two, :], in_=acy[:, two, :])
+            nc.scalar.activation(out=squashed[:, two, :], in_=acy[:, two, :], func=ACT.Tanh)
 
         def hidden_output(pair):
-            both = slice(2 * pair, 2 * pair + 2)
+            two = both(pair)
             nc.vector.tensor_mul(
-                out=ada[:, both, :], in0=out_gate[:, both, :], in1=squashed[:, both, :]
+                out=ada[:, two, :], in0=out_gate[:, two, :], in1=squashed[:, two, :]
             )
-            nc.sync.dma_start(out=ada_rows[:, both, :], in_=ada[:, both, :])
+            nc.sync.dma_start(out=ada_rows[:, two, :], in_=ada[:, two, :])
 
-        hidden_product(0)
-        gain_h_ps = psum.tile([P, GATES], BF16, tag="ig")
+        gain_h_ps = psum.tile([P, GATES], BF16, tag="bank")
         spread(gain_h_ps[:], 0)
         flip(0)
-        hidden_statistics(0)
+        for t in range(TILES):
+            hidden_product(t)
         gain_h = keep.tile([P, GATES], BF16)
         nc.vector.tensor_copy(out=gain_h[:], in_=gain_h_ps[:])
-        hidden_centre(0)
-        hidden_product(1)
-        gains_ps = fixed.tile([P, GATES + 2 * AH], BF16)
-        spread(gains_ps[:, 0:GATES], 1)
-        shift_ps = fixed.tile([P, GATES], F32)
-        spread(shift_ps[:], 2)
-        flip(1)
-        flip(2)
-        input_product(0)
-        hidden_statistics(1)
-        hg_var_eps = keep.tile([P, TILES], F32)
-        nc.vector.tensor_scalar_add(out=hg_var_eps[:], in0=hg_mean_var[:, :, 1], scalar1=EPS)
-        hg_rstd = rstd_of(hg_var_eps[:], TILES, "hg_rstd")
-        hidden_centre(1)
-        flip(3)
-        input_product(1)
-        input_statistics(0)
-        input_product(2)
-        input_product(3)
-        input_statistics(1)
-        for t in range(TILES):
-            hidden_finish(t)
 
-        cell_cols_ps = psum.tile([P, P], BF16, tag="hg")
+        hidden_sums(0)
+        hidden_statistics(0)
+        quantise(0)
+        hidden_centre(0)
+        flip(1)
+        input_product(0)
+        gains_ps = psum.tile([P, GATES + 2 * AH], BF16, tag="bank")
+        spread(gains_ps[:, 0:GATES], 1)
+        shift_ps = psum.tile([P, GATES], F32, tag="bank")
+        spread(shift_ps[:], 2)
+        gain_i = keep.tile([P, GATES], BF16)
+        nc.scalar.copy(out=gain_i[:], in_=gains_ps[:, 0:GATES])
+
+        hidden_sums(1)
+        quantise(1)
+        flip(2)
+        input_product(1)
+        hidden_statistics(1)
+        hidden_centre(1)
+        input_means(0)
+
+        flip(3)
+        quantise(2)
+        input_product(2)
+        hidden_finish(0)
+        input_deviations(0)
+
+        quantise(3)
+        input_product(3)
+        hidden_finish(1)
+        input_means(1)
+        input_deviations(1)
+
+        cell_cols_ps = turn.tile([P, P], BF16, tag="flipped")
         nc.tensor.transpose(cell_cols_ps[:], cell_rows[:], ident_bf16[:])
         cell_cols = keep.tile([P, 2], BF16)
         nc.vector.tensor_copy(out=cell_cols[:], in_=cell_cols_ps[:, 0:2])

@@ -269,20 +269,28 @@ def tile_adaptivelstmcell_pa_kernel(
                 out=out_gate[:, two, :], in_=pre[:, two, 3 * AH : 4 * AH], func=ACT.Sigmoid
             )
 
+        def keep_old(pair):
+            two = both(pair)
+            nc.gpsimd.tensor_tensor(
+                out=kept[:, two, :], in0=in_forget[:, two, AH : 2 * AH], in1=ac_sb[:, two, :],
+                op=ALU.mult,
+            )
+
         def new_cell(pair):
             two = both(pair)
-            nc.vector.tensor_mul(
-                out=kept[:, two, :], in0=in_forget[:, two, AH : 2 * AH], in1=ac_sb[:, two, :]
-            )
             nc.vector.tensor_mul(
                 out=fresh[:, two, :], in0=in_forget[:, two, 0:AH], in1=candidate[:, two, :]
             )
             nc.vector.tensor_add(out=raw[:, two, :], in0=kept[:, two, :], in1=fresh[:, two, :])
+
+        def cell_statistics(pair):
             for t in tiles_of(pair):
                 nc.vector.bn_stats(out=cell_stats[:, t, :], in_=raw[:, t, :])
             for t in tiles_of(pair):
                 nc.vector.bn_aggr(out=cell_mean_var[:, t, :], in_=cell_stats[:, t, :])
-            cell_rstd[pair] = rstd_of(cell_mean_var[:, two, 1], 1.0, "cell_rstd%d" % pair)
+            cell_rstd[pair] = rstd_of(cell_mean_var[:, both(pair), 1], 1.0, "cell_rstd%d" % pair)
+
+        def cell_centre(pair):
             for t in tiles_of(pair):
                 nc.vector.scalar_tensor_tensor(
                     out=cell_centred[:, t, :], in0=raw[:, t, :], scalar=cell_mean_var[:, t, 0:1],
@@ -314,6 +322,10 @@ def tile_adaptivelstmcell_pa_kernel(
             hidden_product(t)
         gain_h = keep.tile([P, GATES], BF16)
         nc.vector.tensor_copy(out=gain_h[:], in_=gain_h_ps[:])
+        gains_ps = psum.tile([P, GATES + 2 * AH], BF16, tag="bank")
+        spread(gains_ps[:, 0:GATES], 1)
+        gain_i = keep.tile([P, GATES], BF16)
+        nc.scalar.copy(out=gain_i[:], in_=gains_ps[:, 0:GATES])
 
         hidden_sums(0)
         hidden_statistics(0)
@@ -321,12 +333,8 @@ def tile_adaptivelstmcell_pa_kernel(
         hidden_centre(0)
         flip(1)
         input_product(0)
-        gains_ps = psum.tile([P, GATES + 2 * AH], BF16, tag="bank")
-        spread(gains_ps[:, 0:GATES], 1)
         shift_ps = psum.tile([P, GATES], F32, tag="bank")
         spread(shift_ps[:], 2)
-        gain_i = keep.tile([P, GATES], BF16)
-        nc.scalar.copy(out=gain_i[:], in_=gains_ps[:, 0:GATES])
 
         hidden_sums(1)
         quantise(1)
@@ -362,8 +370,12 @@ def tile_adaptivelstmcell_pa_kernel(
         for pair in range(2):
             gates(pair)
         for pair in range(2):
-            new_cell(pair)
+            keep_old(pair)
         for pair in range(2):
+            new_cell(pair)
+            cell_statistics(pair)
+        for pair in range(2):
+            cell_centre(pair)
             cell_output(pair)
         for pair in range(2):
             hidden_output(pair)

@@ -111,6 +111,11 @@ def tile_adaptivelstmcell_pa_kernel(
         def spread(out, block):
             nc.tensor.matmul(out=out, lhsT=ones[:], rhs=vec_rows[:, block, :], start=True, stop=True)
 
+        def root_of(var_eps, name):
+            rstd = keep.tile([P, 2], F32, name=name)
+            nc.gpsimd.tensor_tensor(out=rstd[:], in0=var_eps, in1=neg_half[:], op=ALU.pow)
+            return rstd
+
         def rstd_of(squares, scale, name):
             var_eps = keep.tile([P, 2], F32, name=name + "_var_eps")
             nc.gpsimd.tensor_scalar(
@@ -127,7 +132,9 @@ def tile_adaptivelstmcell_pa_kernel(
             return slice(2 * pair, 2 * pair + 2)
 
         hg_ps = {}
-        hg_stats = keep.tile([P, TILES, 6], F32)
+        hg_stats = keep.tile([P, TILES, 9], F32)
+        nc.vector.memset(hg_stats[:, :, 6:8], 0.0)
+        nc.vector.memset(hg_stats[:, :, 8:9], GATES * EPS)
         hg_mean_var = keep.tile([P, TILES, 2], F32)
         hg_rstd = {}
         hg_centred = keep.tile([P, TILES, GATES], F32)
@@ -139,12 +146,12 @@ def tile_adaptivelstmcell_pa_kernel(
 
         def hidden_sums(pair):
             for t in tiles_of(pair):
-                nc.vector.bn_stats(out=hg_stats[:, t, :], in_=hg_ps[t][:])
+                nc.vector.bn_stats(out=hg_stats[:, t, 0:6], in_=hg_ps[t][:])
 
         def hidden_statistics(pair):
             for t in tiles_of(pair):
                 nc.vector.bn_aggr(out=hg_mean_var[:, t, :], in_=hg_stats[:, t, :])
-            hg_rstd[pair] = rstd_of(hg_mean_var[:, both(pair), 1], 1.0, "hg_rstd%d" % pair)
+            hg_rstd[pair] = root_of(hg_mean_var[:, both(pair), 1], "hg_rstd%d" % pair)
 
         def hidden_centre(pair):
             for t in tiles_of(pair):
@@ -236,7 +243,9 @@ def tile_adaptivelstmcell_pa_kernel(
         kept = keep.tile([P, TILES, AH], F32)
         fresh = keep.tile([P, TILES, AH], F32)
         raw = keep.tile([P, TILES, AH], F32)
-        cell_stats = keep.tile([P, TILES, 6], F32)
+        cell_stats = keep.tile([P, TILES, 9], F32)
+        nc.vector.memset(cell_stats[:, :, 6:8], 0.0)
+        nc.vector.memset(cell_stats[:, :, 8:9], AH * EPS)
         cell_mean_var = keep.tile([P, TILES, 2], F32)
         cell_rstd = {}
         cell_centred = keep.tile([P, TILES, AH], F32)
@@ -285,10 +294,10 @@ def tile_adaptivelstmcell_pa_kernel(
 
         def cell_statistics(pair):
             for t in tiles_of(pair):
-                nc.vector.bn_stats(out=cell_stats[:, t, :], in_=raw[:, t, :])
+                nc.vector.bn_stats(out=cell_stats[:, t, 0:6], in_=raw[:, t, :])
             for t in tiles_of(pair):
                 nc.vector.bn_aggr(out=cell_mean_var[:, t, :], in_=cell_stats[:, t, :])
-            cell_rstd[pair] = rstd_of(cell_mean_var[:, both(pair), 1], 1.0, "cell_rstd%d" % pair)
+            cell_rstd[pair] = root_of(cell_mean_var[:, both(pair), 1], "cell_rstd%d" % pair)
 
         def cell_centre(pair):
             for t in tiles_of(pair):

@@ -118,12 +118,8 @@ def tile_adaptivelstmcell_pa_kernel(
 
         def rstd_of(squares, scale, name):
             var_eps = keep.tile([P, 2], F32, name=name + "_var_eps")
-            nc.gpsimd.tensor_scalar(
-                out=var_eps[:], in0=squares, scalar1=scale, scalar2=EPS, op0=ALU.mult, op1=ALU.add
-            )
-            rstd = keep.tile([P, 2], F32, name=name)
-            nc.gpsimd.tensor_tensor(out=rstd[:], in0=var_eps[:], in1=neg_half[:], op=ALU.pow)
-            return rstd
+            nc.scalar.activation(out=var_eps[:], in_=squares, func=ACT.Copy, scale=scale, bias=EPS)
+            return root_of(var_eps[:], name)
 
         def tiles_of(pair):
             return (2 * pair, 2 * pair + 1)
@@ -367,6 +363,9 @@ def tile_adaptivelstmcell_pa_kernel(
 
         cell_cols_ps = turn.tile([P, P], BF16, tag="flipped")
         nc.tensor.transpose(cell_cols_ps[:], cell_rows[:], ident_bf16[:])
+
+        for pair in range(2):
+            gates(pair)
         cell_cols = keep.tile([P, 2], BF16)
         nc.vector.tensor_copy(out=cell_cols[:], in_=cell_cols_ps[:, 0:2])
         for c in range(2):
@@ -375,9 +374,6 @@ def tile_adaptivelstmcell_pa_kernel(
                 cell_cols[:, c : c + 1].to_broadcast([P, P]),
                 ident_bf16[:],
             )
-
-        for pair in range(2):
-            gates(pair)
         for pair in range(2):
             keep_old(pair)
         for pair in range(2):

@@ -282,11 +282,10 @@ def tile_adaptivelstmcell_pa_kernel(
             )
 
         def new_cell(pair):
-            two = both(pair)
-            nc.vector.tensor_mul(
-                out=fresh[:, two, :], in0=in_forget[:, two, 0:AH], in1=candidate[:, two, :]
-            )
-            nc.vector.tensor_add(out=raw[:, two, :], in0=kept[:, two, :], in1=fresh[:, two, :])
+            for t in tiles_of(pair):
+                nc.vector.tensor_mul(out=fresh[:, t, :], in0=in_forget[:, t, 0:AH], in1=candidate[:, t, :])
+            for t in tiles_of(pair):
+                nc.vector.tensor_add(out=raw[:, t, :], in0=kept[:, t, :], in1=fresh[:, t, :])
 
         def cell_statistics(pair):
             for t in tiles_of(pair):
@@ -311,13 +310,13 @@ def tile_adaptivelstmcell_pa_kernel(
                     in1=gains_ps[:, GATES + AH : GATES + 2 * AH], op0=ALU.mult, op1=ALU.add,
                 )
             nc.sync.dma_start(out=acy_rows[:, two, :], in_=acy[:, two, :])
-            nc.scalar.activation(out=squashed[:, two, :], in_=acy[:, two, :], func=ACT.Tanh)
+            for t in tiles_of(pair):
+                nc.scalar.activation(out=squashed[:, t, :], in_=acy[:, t, :], func=ACT.Tanh)
 
         def hidden_output(pair):
             two = both(pair)
-            nc.vector.tensor_mul(
-                out=ada[:, two, :], in0=out_gate[:, two, :], in1=squashed[:, two, :]
-            )
+            for t in tiles_of(pair):
+                nc.vector.tensor_mul(out=ada[:, t, :], in0=out_gate[:, t, :], in1=squashed[:, t, :])
             nc.sync.dma_start(out=ada_rows[:, two, :], in_=ada[:, two, :])
 
         gain_h_ps = psum.tile([P, GATES], BF16, tag="bank")

@@ -41,7 +41,13 @@ def tile_adaptivelstmcell_pa_kernel(
         make_identity(nc, ident_bf16[:])
         ident_f32 = keep.tile([P, P], F32)
         make_identity(nc, ident_f32[:])
-        neg_half = keep.tile([P, 2], F32)
+        w_planes = keep.tile([P, PASSES, GATES], U8, align_bytes=64)
+        nc.vector.memset(w_planes[:].bitcast(I32), 0)
+        vec_rows = keep.tile([P, 3, GATES], BF16)
+        nc.vector.memset(vec_rows[:].rearrange("p v n -> p (v n)").bitcast(I32), 0)
+        cell_rows = keep.tile([P, P], BF16)
+        nc.vector.memset(cell_rows[:].bitcast(I32), 0)
+        neg_half = keep.tile([P, TILES], F32)
         nc.vector.memset(neg_half[:], -0.5)
         ones = keep.tile([P, P], BF16)
         nc.vector.memset(ones[:], 1.0)
@@ -51,8 +57,6 @@ def tile_adaptivelstmcell_pa_kernel(
         ah_sb = keep.tile([P, TILES, AH], BF16)
         nc.scalar.dma_start(out=ah_sb[:], in_=ah.rearrange("(p t) k -> p t k", t=TILES))
 
-        vec_rows = keep.tile([P, 3, GATES], BF16)
-        nc.vector.memset(vec_rows[:], 0.0)
         for row, block, vec in ((0, 0, a_ln_h_w), (0, 2, a_ln_i_b), (1, 2, a_ln_h_b), (0, 1, a_ln_i_w)):
             nc.scalar.dma_start(
                 out=vec_rows[row : row + 1, block, :], in_=vec.rearrange("(r c) -> r c", r=1)
@@ -69,8 +73,6 @@ def tile_adaptivelstmcell_pa_kernel(
             nc.sync.dma_start(out=ai_sb[t][:, IN:K], in_=hx_rows[:, t, :])
 
         load_ai(0)
-        w_planes = keep.tile([P, PASSES, GATES], U8, align_bytes=64)
-        nc.vector.memset(w_planes[:].bitcast(I32), 0)
         scale_rows = a_w_ih_scales.bitcast(I32)
         for quad in range(4):
             nc.sync.dma_start(
@@ -85,8 +87,6 @@ def tile_adaptivelstmcell_pa_kernel(
         for t in range(1, TILES):
             load_ai(t)
 
-        cell_rows = keep.tile([P, P], BF16)
-        nc.vector.memset(cell_rows[:], 0.0)
         for row, vec in ((0, a_ln_c_w), (1, a_ln_c_b)):
             nc.gpsimd.dma_start(
                 out=cell_rows[row : row + 1, :], in_=vec.rearrange("(r c) -> r c", r=1)
@@ -112,8 +112,9 @@ def tile_adaptivelstmcell_pa_kernel(
             nc.tensor.matmul(out=out, lhsT=ones[:], rhs=vec_rows[:, block, :], start=True, stop=True)
 
         def root_of(var_eps, name):
-            rstd = keep.tile([P, 2], F32, name=name)
-            nc.gpsimd.tensor_tensor(out=rstd[:], in0=var_eps, in1=neg_half[:], op=ALU.pow)
+            n = var_eps.shape[1]
+            rstd = keep.tile([P, n], F32, name=name)
+            nc.gpsimd.tensor_tensor(out=rstd[:], in0=var_eps, in1=neg_half[:, 0:n], op=ALU.pow)
             return rstd
 
         def rstd_of(squares, scale, name):
@@ -147,7 +148,8 @@ def tile_adaptivelstmcell_pa_kernel(
         def hidden_statistics(pair):
             for t in tiles_of(pair):
                 nc.vector.bn_aggr(out=hg_mean_var[:, t, :], in_=hg_stats[:, t, :])
-            hg_rstd[pair] = root_of(hg_mean_var[:, both(pair), 1], "hg_rstd%d" % pair)
+            if pair == 1:
+                hg_rstd[0] = root_of(hg_mean_var[:, :, 1], "hg_rstd")
 
         def hidden_centre(pair):
             for t in tiles_of(pair):
@@ -160,7 +162,7 @@ def tile_adaptivelstmcell_pa_kernel(
             for t in tiles_of(pair):
                 nc.vector.scalar_tensor_tensor(
                     out=hidden[:, t, :], in0=hg_centred[:, t, :],
-                    scalar=hg_rstd[pair][:, t % 2 : t % 2 + 1],
+                    scalar=hg_rstd[0][:, t : t + 1],
                     in1=shift_ps[:], op0=ALU.mult, op1=ALU.add,
                 )
 

@@ -41,14 +41,14 @@ def tile_adaptivelstmcell_pa_kernel(
         make_identity(nc, ident_bf16[:])
         ident_f32 = keep.tile([P, P], F32)
         make_identity(nc, ident_f32[:])
+        neg_half = keep.tile([P, TILES], F32)
+        nc.vector.memset(neg_half[:], -0.5)
         w_planes = keep.tile([P, PASSES, GATES], U8, align_bytes=64)
         nc.vector.memset(w_planes[:].bitcast(I32), 0)
         vec_rows = keep.tile([P, 3, GATES], BF16)
         nc.vector.memset(vec_rows[:].rearrange("p v n -> p (v n)").bitcast(I32), 0)
         cell_rows = keep.tile([P, P], BF16)
         nc.vector.memset(cell_rows[:].bitcast(I32), 0)
-        neg_half = keep.tile([P, TILES], F32)
-        nc.vector.memset(neg_half[:], -0.5)
         ones = keep.tile([P, P], BF16)
         nc.vector.memset(ones[:], 1.0)
 
@@ -56,6 +56,8 @@ def tile_adaptivelstmcell_pa_kernel(
         nc.scalar.dma_start(out=whh_sb[:], in_=a_w_hh.rearrange("(c p) k -> p c k", p=P))
         ah_sb = keep.tile([P, TILES, AH], BF16)
         nc.scalar.dma_start(out=ah_sb[:], in_=ah.rearrange("(p t) k -> p t k", t=TILES))
+        warm = keep.tile([P, 1], F32)
+        nc.scalar.activation(out=warm[:], in_=neg_half[:, 0:1], func=ACT.Sigmoid)
 
         for row, block, vec in ((0, 0, a_ln_h_w), (0, 2, a_ln_i_b), (1, 2, a_ln_h_b), (0, 1, a_ln_i_w)):
             nc.scalar.dma_start(
@@ -93,9 +95,6 @@ def tile_adaptivelstmcell_pa_kernel(
             )
         ac_sb = keep.tile([P, TILES, AH], BF16)
         nc.gpsimd.dma_start(out=ac_sb[:], in_=ac.rearrange("(p t) n -> p t n", t=TILES))
-
-        warm = keep.tile([P, 1], F32)
-        nc.scalar.activation(out=warm[:], in_=neg_half[:, 0:1], func=ACT.Sigmoid)
 
         whhT_ps = psum.tile([P, 4, AH], BF16, tag="bank")
         for c in range(4):

@@ -21,6 +21,7 @@ PASSES = K // K_PASS
 AH = 128
 GATES = 4 * AH
 EPS = 1e-5
+WARM_UP = 5
 
 FLOPS = 2 * BATCH * GATES * K + 2 * BATCH * GATES * AH
 
@@ -37,6 +38,13 @@ def tile_adaptivelstmcell_pa_kernel(
             tc.psum_pool(name="psum", bufs=6) as psum, \
             tc.manual_schedule():
 
+        ones_f32 = keep.tile([P, P], F32)
+        nc.vector.memset(ones_f32[:], 1.0)
+        warm_ps = turn.tile([P, 2, 2, P], F32, tag="flipped")
+        for i in range(WARM_UP):
+            nc.tensor.matmul(
+                out=warm_ps[:, 0, 0, :], lhsT=ones_f32[:], rhs=ones_f32[:], start=True, stop=True
+            )
         ident_bf16 = keep.tile([P, P], BF16)
         make_identity(nc, ident_bf16[:])
         ident_f32 = keep.tile([P, P], F32)
@@ -45,7 +53,9 @@ def tile_adaptivelstmcell_pa_kernel(
         nc.vector.memset(neg_half[:], -0.5)
         w_planes = keep.tile([P, PASSES, GATES], U8, align_bytes=64)
         nc.vector.memset(w_planes[:].bitcast(I32), 0)
-        vec_rows = keep.tile([P, 3, GATES], BF16)
+        shift_rows = keep.tile([P, P], BF16)
+        nc.vector.memset(shift_rows[:].bitcast(I32), 0)
+        vec_rows = keep.tile([P, 2, GATES], BF16)
         nc.vector.memset(vec_rows[:].rearrange("p v n -> p (v n)").bitcast(I32), 0)
         cell_rows = keep.tile([P, P], BF16)
         nc.vector.memset(cell_rows[:].bitcast(I32), 0)
@@ -59,10 +69,12 @@ def tile_adaptivelstmcell_pa_kernel(
         warm = keep.tile([P, 1], F32)
         nc.scalar.activation(out=warm[:], in_=neg_half[:, 0:1], func=ACT.Sigmoid)
 
-        for row, block, vec in ((0, 0, a_ln_h_w), (0, 2, a_ln_i_b), (1, 2, a_ln_h_b), (0, 1, a_ln_i_w)):
+        nc.scalar.dma_start(out=vec_rows[0:1, 0, :], in_=a_ln_h_w.rearrange("(r c) -> r c", r=1))
+        for v, vec in enumerate((a_ln_i_b, a_ln_h_b)):
             nc.scalar.dma_start(
-                out=vec_rows[row : row + 1, block, :], in_=vec.rearrange("(r c) -> r c", r=1)
+                out=shift_rows[4 * v : 4 * v + 4, :], in_=vec.rearrange("(c n) -> c n", c=4)
             )
+        nc.scalar.dma_start(out=vec_rows[0:1, 1, :], in_=a_ln_i_w.rearrange("(r c) -> r c", r=1))
 
         x_rows = x.rearrange("(p t) k -> p t k", t=TILES)
         hx_rows = hx.rearrange("(p t) k -> p t k", t=TILES)
@@ -321,25 +333,38 @@ def tile_adaptivelstmcell_pa_kernel(
             nc.sync.dma_start(out=ada_rows[:, two, :], in_=ada[:, two, :])
 
         gain_h_ps = psum.tile([P, GATES], BF16, tag="bank")
-        spread(gain_h_ps[:], 0)
         flip(0)
         for t in range(TILES):
             hidden_product(t)
+        spread(gain_h_ps[:], 0)
         gain_h = keep.tile([P, GATES], BF16)
-        nc.vector.tensor_copy(out=gain_h[:], in_=gain_h_ps[:])
+        shift_cols_ps = turn.tile([P, P], BF16, tag="flipped")
+        nc.tensor.transpose(shift_cols_ps[:], shift_rows[:], ident_bf16[:])
+        both_shifts = keep.tile([P, 8], F32)
+        nc.scalar.copy(out=both_shifts[:], in_=shift_cols_ps[:, 0:8])
+        shift_cols = keep.tile([P, 4], F32)
+        nc.gpsimd.tensor_tensor(
+            out=shift_cols[:], in0=both_shifts[:, 0:4], in1=both_shifts[:, 4:8], op=ALU.add
+        )
         gains_ps = psum.tile([P, GATES + 2 * AH], BF16, tag="bank")
         spread(gains_ps[:, 0:GATES], 1)
         gain_i = keep.tile([P, GATES], BF16)
         nc.scalar.copy(out=gain_i[:], in_=gains_ps[:, 0:GATES])
 
         hidden_sums(0)
+        nc.vector.tensor_copy(out=gain_h[:], in_=gain_h_ps[:])
         hidden_statistics(0)
         quantise(0)
         hidden_centre(0)
         flip(1)
         input_product(0)
         shift_ps = psum.tile([P, GATES], F32, tag="bank")
-        spread(shift_ps[:], 2)
+        for c in range(4):
+            nc.tensor.transpose(
+                shift_ps[:, c * AH : (c + 1) * AH],
+                shift_cols[:, c : c + 1].to_broadcast([P, P]),
+                ident_f32[:],
+            )
 
         hidden_sums(1)
         quantise(1)

@@ -208,11 +208,13 @@ def tile_adaptivelstmcell_pa_kernel(
         def quantise(t):
             codes[t] = rows.tile([P, PASSES, P], U32, name="codes", align_bytes=64)
             planes[t] = rows.tile([P, PASSES, P], U8, name="planes", align_bytes=64)
-            nc.vector.quantize_mx(
-                out=codes[t][:].rearrange("p g b -> p (g b)").bitcast(FP8X4),
-                scales=planes[t][:].rearrange("p g b -> p (g b)"),
-                in_=grouped[t][:].rearrange("p g b t -> p (g b t)"),
-            )
+            for half in range(2):
+                two = slice(2 * half, 2 * half + 2)
+                nc.vector.quantize_mx(
+                    out=codes[t][:, two, :].rearrange("p g b -> p (g b)").bitcast(FP8X4),
+                    scales=planes[t][:, two, :].rearrange("p g b -> p (g b)"),
+                    in_=grouped[t][:, two, :, :].rearrange("p g b t -> p (g b t)"),
+                )
 
         def input_product(t):
             ig_ps[t] = psum.tile([P, GATES], F32, tag="bank", name="ig_ps")

@@ -185,10 +185,11 @@ def tile_adaptivelstmcell_pa_kernel(
         ig_squares = keep.tile([P, TILES], F32)
         ig_rstd = {}
 
-        def flip(t):
-            grouped[t] = rows.tile([P, PASSES, P, 4], BF16, name="grouped", align_bytes=64)
+        def flip(t, halves=(0, 1)):
+            if 0 in halves:
+                grouped[t] = rows.tile([P, PASSES, P, 4], BF16, name="grouped", align_bytes=64)
             pairs = ai_sb[t][:].bitcast(F32)
-            for half in range(2):
+            for half in halves:
                 flipped = turn.tile([P, 2, 2, P], F32)
                 for g2 in range(2):
                     g = 2 * half + g2
@@ -335,9 +336,12 @@ def tile_adaptivelstmcell_pa_kernel(
             nc.sync.dma_start(out=ada_rows[:, two, :], in_=ada[:, two, :])
 
         gain_h_ps = psum.tile([P, GATES], BF16, tag="bank")
-        flip(0)
-        for t in range(TILES):
-            hidden_product(t)
+        flip(0, (0,))
+        hidden_product(0)
+        hidden_product(1)
+        flip(0, (1,))
+        hidden_product(2)
+        hidden_product(3)
         spread(gain_h_ps[:], 0)
         gain_h = keep.tile([P, GATES], BF16)
         shift_cols_ps = turn.tile([P, P], BF16, tag="flipped")
@@ -354,9 +358,9 @@ def tile_adaptivelstmcell_pa_kernel(
         nc.scalar.copy(out=gain_i[:], in_=gains_ps[:, 0:GATES])
 
         hidden_sums(0)
-        nc.vector.tensor_copy(out=gain_h[:], in_=gain_h_ps[:])
         hidden_statistics(0)
         quantise(0)
+        nc.vector.tensor_copy(out=gain_h[:], in_=gain_h_ps[:])
         hidden_centre(0)
         flip(1)
         input_product(0)

import concourse.mybir as mybir
from concourse.masks import make_identity

F32 = mybir.dt.float32
BF16 = mybir.dt.bfloat16
I32 = mybir.dt.int32
U32 = mybir.dt.uint32
U8 = mybir.dt.uint8
FP8X4 = mybir.dt.float8_e4m3fn_x4
FP4X4 = mybir.dt.float4_e2m1fn_x4
ALU = mybir.AluOpType
ACT = mybir.ActivationFunctionType

P = 128
BATCH = 512
TILES = BATCH // P
IN = 1024
K = 2 * IN
K_PASS = 512
PASSES = K // K_PASS
AH = 128
GATES = 4 * AH
EPS = 1e-5
WARM_UP = 5

FLOPS = 2 * BATCH * GATES * K + 2 * BATCH * GATES * AH


def tile_adaptivelstmcell_pa_kernel(
    tc, x, hx, ah, ac, a_w_ih_words, a_w_ih_scales, a_w_hh,
    a_ln_i_w, a_ln_i_b, a_ln_h_w, a_ln_h_b, a_ln_c_w, a_ln_c_b, out_0, out_1,
):
    nc = tc.nc
    with tc.tile_pool(name="keep", bufs=1) as keep, \
            tc.tile_pool(name="rows", bufs=TILES) as rows, \
            tc.tile_pool(name="work", bufs=3) as work, \
            tc.psum_pool(name="turn", bufs=2) as turn, \
            tc.psum_pool(name="psum", bufs=6) as psum, \
            tc.manual_schedule():

        ones_f32 = keep.tile([P, P], F32)
        nc.vector.memset(ones_f32[:], 1.0)
        warm_ps = turn.tile([P, 2, 2, P], F32, tag="flipped")
        for i in range(WARM_UP):
            nc.tensor.matmul(
                out=warm_ps[:, 0, 0, :], lhsT=ones_f32[:], rhs=ones_f32[:], start=True, stop=True
            )
        ident_bf16 = keep.tile([P, P], BF16)
        make_identity(nc, ident_bf16[:])
        ident_f32 = keep.tile([P, P], F32)
        make_identity(nc, ident_f32[:])
        neg_half = keep.tile([P, TILES], F32)
        nc.vector.memset(neg_half[:], -0.5)
        w_planes = keep.tile([P, PASSES, GATES], U8, align_bytes=64)
        nc.vector.memset(w_planes[:].bitcast(I32), 0)
        shift_rows = keep.tile([P, P], BF16)
        nc.vector.memset(shift_rows[:].bitcast(I32), 0)
        vec_rows = keep.tile([P, 2, GATES], BF16)
        nc.vector.memset(vec_rows[:].rearrange("p v n -> p (v n)").bitcast(I32), 0)
        cell_rows = keep.tile([P, P], BF16)
        nc.vector.memset(cell_rows[:].bitcast(I32), 0)
        ones = keep.tile([P, P], BF16)
        nc.vector.memset(ones[:], 1.0)

        whh_sb = keep.tile([P, 4, AH], BF16)
        nc.scalar.dma_start(out=whh_sb[:], in_=a_w_hh.rearrange("(c p) k -> p c k", p=P))
        ah_sb = keep.tile([P, TILES, AH], BF16)
        nc.scalar.dma_start(out=ah_sb[:], in_=ah.rearrange("(p t) k -> p t k", t=TILES))
        warm = keep.tile([P, 1], F32)
        nc.scalar.activation(out=warm[:], in_=neg_half[:, 0:1], func=ACT.Sigmoid)

        nc.scalar.dma_start(out=vec_rows[0:1, 0, :], in_=a_ln_h_w.rearrange("(r c) -> r c", r=1))
        for v, vec in enumerate((a_ln_i_b, a_ln_h_b)):
            nc.scalar.dma_start(
                out=shift_rows[4 * v : 4 * v + 4, :], in_=vec.rearrange("(c n) -> c n", c=4)
            )
        nc.scalar.dma_start(out=vec_rows[0:1, 1, :], in_=a_ln_i_w.rearrange("(r c) -> r c", r=1))

        x_rows = x.rearrange("(p t) k -> p t k", t=TILES)
        hx_rows = hx.rearrange("(p t) k -> p t k", t=TILES)
        ai_sb = []
        for t in range(TILES):
            ai_sb.append(rows.tile([P, K], BF16, name="ai_sb"))

        def load_ai(t):
            nc.sync.dma_start(out=ai_sb[t][:, 0:IN], in_=x_rows[:, t, :])
            nc.sync.dma_start(out=ai_sb[t][:, IN:K], in_=hx_rows[:, t, :])

        load_ai(0)
        scale_rows = a_w_ih_scales.bitcast(I32)
        for quad in range(4):
            nc.sync.dma_start(
                out=w_planes[32 * quad : 32 * quad + 4, :, :].bitcast(I32),
                in_=scale_rows[:, 4 * quad : 4 * quad + 4, :].rearrange("g r n -> r g n"),
            )
        w_sb = keep.tile([P, PASSES, 2 * GATES], U8, align_bytes=64)
        nc.sync.dma_start(
            out=w_sb[:].bitcast(I32),
            in_=a_w_ih_words.bitcast(I32).rearrange("g p n -> p g n"),
        )
        for t in range(1, TILES):
            load_ai(t)

        for row, vec in ((0, a_ln_c_w), (1, a_ln_c_b)):
            nc.gpsimd.dma_start(
                out=cell_rows[row : row + 1, :], in_=vec.rearrange("(r c) -> r c", r=1)
            )
        ac_sb = keep.tile([P, TILES, AH], BF16)
        nc.gpsimd.dma_start(out=ac_sb[:], in_=ac.rearrange("(p t) n -> p t n", t=TILES))

        whhT_ps = psum.tile([P, 4, AH], BF16, tag="bank")
        for c in range(4):
            nc.tensor.transpose(whhT_ps[:, c, :], whh_sb[:, c, :], ident_bf16[:])
        ahT_ps = psum.tile([P, TILES, P], BF16, tag="bank")
        for t in range(TILES):
            nc.tensor.transpose(ahT_ps[:, t, :], ah_sb[:, t, :], ident_bf16[:])
        whhT = keep.tile([P, GATES], BF16)
        nc.vector.tensor_copy(out=whhT[:], in_=whhT_ps[:].rearrange("p c n -> p (c n)"))
        ahT = keep.tile([P, TILES, P], BF16)
        nc.scalar.copy(out=ahT[:], in_=ahT_ps[:])

        def spread(out, block):
            nc.tensor.matmul(out=out, lhsT=ones[:], rhs=vec_rows[:, block, :], start=True, stop=True)

        def root_of(var_eps, name):
            n = var_eps.shape[1]
            rstd = keep.tile([P, n], F32, name=name)
            nc.gpsimd.tensor_tensor(out=rstd[:], in0=var_eps, in1=neg_half[:, 0:n], op=ALU.pow)
            return rstd

        def rstd_of(squares, scale, name):
            var_eps = keep.tile([P, 2], F32, name=name + "_var_eps")
            nc.scalar.activation(out=var_eps[:], in_=squares, func=ACT.Copy, scale=scale, bias=EPS)
            return root_of(var_eps[:], name)

        def tiles_of(pair):
            return (2 * pair, 2 * pair + 1)

        def both(pair):
            return slice(2 * pair, 2 * pair + 2)

        hg_ps = {}
        hg_stats = keep.tile([P, TILES, 9], F32)
        nc.vector.memset(hg_stats[:, :, 6:8], 0.0)
        nc.vector.memset(hg_stats[:, :, 8:9], GATES * EPS)
        hg_mean_var = keep.tile([P, TILES, 2], F32)
        hg_rstd = {}
        hg_centred = keep.tile([P, TILES, GATES], F32)
        hidden = keep.tile([P, TILES, GATES], F32)

        def hidden_product(t):
            hg_ps[t] = psum.tile([P, GATES], F32, tag="bank", name="hg_ps")
            nc.tensor.matmul(out=hg_ps[t][:], lhsT=ahT[:, t, :], rhs=whhT[:], start=True, stop=True)

        def hidden_sums(pair):
            for t in tiles_of(pair):
                nc.vector.bn_stats(out=hg_stats[:, t, 0:6], in_=hg_ps[t][:])

        def hidden_statistics(pair):
            for t in tiles_of(pair):
                nc.vector.bn_aggr(out=hg_mean_var[:, t, :], in_=hg_stats[:, t, :])
            if pair == 1:
                hg_rstd[0] = root_of(hg_mean_var[:, :, 1], "hg_rstd")

        def hidden_centre(pair):
            for t in tiles_of(pair):
                nc.vector.scalar_tensor_tensor(
                    out=hg_centred[:, t, :], in0=hg_ps[t][:], scalar=hg_mean_var[:, t, 0:1],
                    in1=gain_h[:], op0=ALU.subtract, op1=ALU.mult,
                )

        def hidden_finish(pair):
            for t in tiles_of(pair):
                nc.vector.scalar_tensor_tensor(
                    out=hidden[:, t, :], in0=hg_centred[:, t, :],
                    scalar=hg_rstd[0][:, t : t + 1],
                    in1=shift_ps[:], op0=ALU.mult, op1=ALU.add,
                )

        grouped = {}
        codes = {}
        planes = {}
        ig_ps = {}
        ig_neg_mean = keep.tile([P, TILES], F32)
        ig_squares = keep.tile([P, TILES], F32)
        ig_rstd = {}

        def flip(t, halves=(0, 1)):
            if 0 in halves:
                grouped[t] = rows.tile([P, PASSES, P, 4], BF16, name="grouped", align_bytes=64)
            pairs = ai_sb[t][:].bitcast(F32)
            for half in halves:
                flipped = turn.tile([P, 2, 2, P], F32)
                for g2 in range(2):
                    g = 2 * half + g2
                    for u in range(2):
                        nc.tensor.transpose(
                            flipped[:, g2, u, :],
                            pairs[:, 256 * g + u : 256 * (g + 1) : 2],
                            ident_f32[:],
                        )
                nc.scalar.copy(
                    out=grouped[t][:, 2 * half : 2 * half + 2, :, :]
                    .rearrange("p g b t -> p (g b t)").bitcast(F32)
                    .rearrange("p (g b u) -> p g b u", g=2, u=2),
                    in_=flipped[:].rearrange("p g u b -> p g b u"),
                )

        def quantise(t):
            codes[t] = rows.tile([P, PASSES, P], U32, name="codes", align_bytes=64)
            planes[t] = rows.tile([P, PASSES, P], U8, name="planes", align_bytes=64)
            for half in range(2):
                two = slice(2 * half, 2 * half + 2)
                nc.vector.quantize_mx(
                    out=codes[t][:, two, :].rearrange("p g b -> p (g b)").bitcast(FP8X4),
                    scales=planes[t][:, two, :].rearrange("p g b -> p (g b)"),
                    in_=grouped[t][:, two, :, :].rearrange("p g b t -> p (g b t)"),
                )

        def input_product(t):
            ig_ps[t] = psum.tile([P, GATES], F32, tag="bank", name="ig_ps")
            for g in range(PASSES):
                nc.tensor.matmul_mx(
                    out=ig_ps[t][:],
                    lhsT=codes[t][:, g, :].bitcast(FP8X4),
                    lhsT_scale=planes[t][:, g, :],
                    rhs=w_sb[:, g, :].bitcast(FP4X4),
                    rhs_scale=w_planes[:, g, :],
                    start=(g == 0),
                    stop=(g == PASSES - 1),
                )

        def input_means(pair):
            for t in tiles_of(pair):
                unused = work.tile([P, GATES], F32, name="unused")
                nc.scalar.activation(
                    out=unused[:], in_=ig_ps[t][:], func=ACT.Identity, scale=-1.0 / GATES,
                    accum_out=ig_neg_mean[:, t : t + 1],
                )

        def input_deviations(pair):
            for t in tiles_of(pair):
                unused = work.tile([P, GATES], F32, name="unused")
                nc.scalar.activation(
                    out=unused[:], in_=ig_ps[t][:], func=ACT.Square, bias=ig_neg_mean[:, t : t + 1],
                    accum_out=ig_squares[:, t : t + 1],
                )
            ig_rstd[pair] = rstd_of(ig_squares[:, both(pair)], 1.0 / GATES, "ig_rstd%d" % pair)

        ig_centred = keep.tile([P, TILES, GATES], F32)
        pre = keep.tile([P, TILES, GATES], F32)
        in_forget = keep.tile([P, TILES, 2 * AH], F32)
        candidate = keep.tile([P, TILES, AH], F32)
        out_gate = keep.tile([P, TILES, AH], F32)
        kept = keep.tile([P, TILES, AH], F32)
        fresh = keep.tile([P, TILES, AH], F32)
        raw = keep.tile([P, TILES, AH], F32)
        cell_stats = keep.tile([P, TILES, 9], F32)
        nc.vector.memset(cell_stats[:, :, 6:8], 0.0)
        nc.vector.memset(cell_stats[:, :, 8:9], AH * EPS)
        cell_mean_var = keep.tile([P, TILES, 2], F32)
        cell_rstd = {}
        cell_centred = keep.tile([P, TILES, AH], F32)
        acy = keep.tile([P, TILES, AH], F32)
        squashed = keep.tile([P, TILES, AH], F32)
        ada = keep.tile([P, TILES, AH], F32)
        ada_rows = out_0.rearrange("(p t) n -> p t n", t=TILES)
        acy_rows = out_1.rearrange("(p t) n -> p t n", t=TILES)

        def gates(pair):
            for t in tiles_of(pair):
                nc.vector.scalar_tensor_tensor(
                    out=ig_centred[:, t, :], in0=ig_ps[t][:], scalar=ig_neg_mean[:, t : t + 1],
                    in1=gain_i[:], op0=ALU.add, op1=ALU.mult,
                )
            for t in tiles_of(pair):
                nc.vector.scalar_tensor_tensor(
                    out=pre[:, t, :], in0=ig_centred[:, t, :],
                    scalar=ig_rstd[pair][:, t % 2 : t % 2 + 1],
                    in1=hidden[:, t, :], op0=ALU.mult, op1=ALU.add,
                )
            two = both(pair)
            nc.scalar.activation(
                out=in_forget[:, two, :], in_=pre[:, two, 0 : 2 * AH], func=ACT.Sigmoid
            )
            nc.scalar.activation(
                out=candidate[:, two, :], in_=pre[:, two, 2 * AH : 3 * AH], func=ACT.Tanh
            )
            nc.scalar.activation(
                out=out_gate[:, two, :], in_=pre[:, two, 3 * AH : 4 * AH], func=ACT.Sigmoid
            )

        def keep_old(pair):
            two = both(pair)
            nc.gpsimd.tensor_tensor(
                out=kept[:, two, :], in0=in_forget[:, two, AH : 2 * AH], in1=ac_sb[:, two, :],
                op=ALU.mult,
            )

        def new_cell(pair):
            for t in tiles_of(pair):
                nc.vector.tensor_mul(out=fresh[:, t, :], in0=in_forget[:, t, 0:AH], in1=candidate[:, t, :])
            for t in tiles_of(pair):
                nc.vector.tensor_add(out=raw[:, t, :], in0=kept[:, t, :], in1=fresh[:, t, :])

        def cell_statistics(pair):
            for t in tiles_of(pair):
                nc.vector.bn_stats(out=cell_stats[:, t, 0:6], in_=raw[:, t, :])
            for t in tiles_of(pair):
                nc.vector.bn_aggr(out=cell_mean_var[:, t, :], in_=cell_stats[:, t, :])
            cell_rstd[pair] = root_of(cell_mean_var[:, both(pair), 1], "cell_rstd%d" % pair)

        def cell_centre(pair):
            for t in tiles_of(pair):
                nc.vector.scalar_tensor_tensor(
                    out=cell_centred[:, t, :], in0=raw[:, t, :], scalar=cell_mean_var[:, t, 0:1],
                    in1=gains_ps[:, GATES : GATES + AH], op0=ALU.subtract, op1=ALU.mult,
                )

        def cell_output(pair):
            two = both(pair)
            for t in tiles_of(pair):
                nc.vector.scalar_tensor_tensor(
                    out=acy[:, t, :], in0=cell_centred[:, t, :],
                    scalar=cell_rstd[pair][:, t % 2 : t % 2 + 1],
                    in1=gains_ps[:, GATES + AH : GATES + 2 * AH], op0=ALU.mult, op1=ALU.add,
                )
            nc.sync.dma_start(out=acy_rows[:, two, :], in_=acy[:, two, :])
            for t in tiles_of(pair):
                nc.scalar.activation(out=squashed[:, t, :], in_=acy[:, t, :], func=ACT.Tanh)

        def hidden_output(pair):
            two = both(pair)
            for t in tiles_of(pair):
                nc.vector.tensor_mul(out=ada[:, t, :], in0=out_gate[:, t, :], in1=squashed[:, t, :])
            nc.sync.dma_start(out=ada_rows[:, two, :], in_=ada[:, two, :])

        gain_h_ps = psum.tile([P, GATES], BF16, tag="bank")
        flip(0, (0,))
        hidden_product(0)
        hidden_product(1)
        flip(0, (1,))
        hidden_product(2)
        hidden_product(3)
        spread(gain_h_ps[:], 0)
        gain_h = keep.tile([P, GATES], BF16)
        shift_cols_ps = turn.tile([P, P], BF16, tag="flipped")
        nc.tensor.transpose(shift_cols_ps[:], shift_rows[:], ident_bf16[:])
        both_shifts = keep.tile([P, 8], F32)
        nc.scalar.copy(out=both_shifts[:], in_=shift_cols_ps[:, 0:8])
        shift_cols = keep.tile([P, 4], F32)
        nc.gpsimd.tensor_tensor(
            out=shift_cols[:], in0=both_shifts[:, 0:4], in1=both_shifts[:, 4:8], op=ALU.add
        )
        gains_ps = psum.tile([P, GATES + 2 * AH], BF16, tag="bank")
        spread(gains_ps[:, 0:GATES], 1)
        gain_i = keep.tile([P, GATES], BF16)
        nc.scalar.copy(out=gain_i[:], in_=gains_ps[:, 0:GATES])

        hidden_sums(0)
        hidden_statistics(0)
        quantise(0)
        nc.vector.tensor_copy(out=gain_h[:], in_=gain_h_ps[:])
        hidden_centre(0)
        flip(1)
        input_product(0)
        shift_ps = psum.tile([P, GATES], F32, tag="bank")
        for c in range(4):
            nc.tensor.transpose(
                shift_ps[:, c * AH : (c + 1) * AH],
                shift_cols[:, c : c + 1].to_broadcast([P, P]),
                ident_f32[:],
            )

        hidden_sums(1)
        quantise(1)
        flip(2)
        input_product(1)
        hidden_statistics(1)
        hidden_centre(1)
        input_means(0)

        flip(3)
        quantise(2)
        input_product(2)
        hidden_finish(0)
        input_deviations(0)

        quantise(3)
        input_product(3)
        hidden_finish(1)
        input_means(1)
        input_deviations(1)

        cell_cols_ps = turn.tile([P, P], BF16, tag="flipped")
        nc.tensor.transpose(cell_cols_ps[:], cell_rows[:], ident_bf16[:])

        for pair in range(2):
            gates(pair)
        cell_cols = keep.tile([P, 2], BF16)
        nc.vector.tensor_copy(out=cell_cols[:], in_=cell_cols_ps[:, 0:2])
        for c in range(2):
            nc.tensor.transpose(
                gains_ps[:, GATES + c * AH : GATES + (c + 1) * AH],
                cell_cols[:, c : c + 1].to_broadcast([P, P]),
                ident_bf16[:],
            )
        for pair in range(2):
            keep_old(pair)
        for pair in range(2):
            new_cell(pair)
            cell_statistics(pair)
        for pair in range(2):
            cell_centre(pair)
            cell_output(pair)
        for pair in range(2):
            hidden_output(pair)
